import numpy as np
import ml_dtypes

BF16 = ml_dtypes.bfloat16


def bf(x):
    return np.asarray(x, np.float32).astype(BF16)


def f32(x):
    return np.asarray(x, np.float32)


def f64(x):
    return np.asarray(x).astype(np.float64)


def striped(idx):
    return np.tile(idx.reshape(-1, 16).T, (8, 1))


C, S, N = 1024, 256, 128


def pos_encoding():
    half = np.arange(C // 2).astype(np.float32)
    inv = np.power(np.float32(10000.0), np.float32(4.0) * half / np.float32(C))
    ang = np.arange(N).astype(np.float32)[:, None] / inv[None, :]
    pe = np.stack([np.sin(f64(ang)), np.cos(f64(ang))], axis=-1).reshape(N, C)
    return f32(np.ascontiguousarray(pe.T))


def setup_inputs():
    return {"emb": f32(np.random.standard_normal((C, S))), "pos": pos_encoding(), "wq": bf(np.random.standard_normal((C, C)) / np.sqrt(C)), "bq": f32(0.1 * np.random.standard_normal((C, 1))), "wk": bf(np.random.standard_normal((C, C)) / np.sqrt(C)), "bk": f32(0.1 * np.random.standard_normal((C, 1))), "offs": striped(np.random.permutation(np.tile(np.arange(S), 2))[:N])}


def reference(emb, pos, wq, bq, wk, bk, offs):
    idx = offs[:16].T.reshape(-1)
    x = f64(emb)[:, idx] + f64(pos)
    q = f64(wq).T @ x + f64(bq)
    k = f64(wk).T @ x + f64(bk)
    return np.concatenate([q, k], axis=0)

@@ -1,0 +1,90 @@
+import concourse.mybir as mybir
+
+P = 128
+C = 1024
+S = 256
+N = 128
+M = 1024
+CB = C // P
+MB = M // P
+PAIRS = CB // 2
+
+FLOPS = 2 * C * 2 * M * N
+
+F32 = mybir.dt.float32
+BF16 = mybir.dt.bfloat16
+U16 = mybir.dt.uint16
+
+
+def tile_transformerclassifier_kernel(tc, emb, pos, wq, bq, wk, bk, offs, out):
+    nc = tc.nc
+    add = mybir.AluOpType.add
+    identity = mybir.ActivationFunctionType.Identity
+
+    emb_blocks = emb.rearrange("(p b) s -> b p s", b=CB)
+    pos_rows = pos.rearrange("(p b) j -> p b j", b=CB)
+    weight_rows = [w.rearrange("(p b) (m g) -> p b m g", b=CB, g=MB) for w in (wq, wk)]
+    bias_rows = [v.rearrange("(p g) o -> p (g o)", g=MB) for v in (bq, bk)]
+    out_rows = out.rearrange("(h p g) j -> h p g j", h=2, g=MB)
+
+    with (
+        tc.tile_pool(name="held", bufs=1) as held,
+        tc.psum_pool(name="banks", bufs=1) as banks,
+    ):
+        def queue_of(i):
+            return nc.sync if i % 2 == 0 else nc.scalar
+
+        def load_weight_pair(h, i):
+            weight = held.tile([P, 2, P, MB], BF16, name=f"weight{h}_{i}")
+            queue_of(i).dma_start(weight[:], weight_rows[h][:, 2 * i : 2 * i + 2])
+            return weight
+
+        offsets = held.tile([P, N // 16], U16, name="offsets")
+        nc.sync.dma_start(offsets[:], offs)
+
+        pos_sb = held.tile([P, CB, N], F32, name="pos_sb")
+        nc.scalar.dma_start(pos_sb[:], pos_rows)
+
+        biases = []
+        for h in range(2):
+            bias = held.tile([P, MB], F32, name=f"bias{h}")
+            nc.gpsimd.dma_start(bias[:], bias_rows[h])
+            biases.append(bias)
+
+        tables = []
+        weights = [[], []]
+        for i in range(PAIRS):
+            for b in (2 * i, 2 * i + 1):
+                table = held.tile([P, S], F32, name=f"table{b}")
+                queue_of(i).dma_start(table[:], emb_blocks[b])
+                tables.append(table)
+            weights[0].append(load_weight_pair(0, i))
+        for i in range(PAIRS):
+            weights[1].append(load_weight_pair(1, i))
+
+        xs = []
+        for b in range(CB):
+            x_f32 = held.tile([P, N], F32, name=f"x_f32_{b}")
+            nc.vector.tensor_tensor(x_f32[:], tables[b][:].indirect(offsets[:]), pos_sb[:, b, :], add)
+            x = held.tile([P, N], BF16, name=f"x{b}")
+            nc.vector.tensor_copy(x[:], x_f32[:])
+            xs.append(x)
+
+        for h in range(2):
+            sums = [banks.tile([P, N], F32, name=f"sum{g}") for g in range(MB)]
+            for b in range(CB):
+                for g in range(MB):
+                    nc.tensor.matmul(
+                        sums[g][:],
+                        weights[h][b // 2][:, b % 2, :, g],
+                        xs[b][:],
+                        start=(b == 0),
+                        stop=(b == CB - 1),
+                    )
+            y = held.tile([P, MB, N], F32, name=f"y{h}")
+            for g in range(MB):
+                if g % 2 == 0:
+                    nc.vector.tensor_scalar(y[:, g, :], sums[g][:], biases[h][:, g : g + 1], None, add)
+                else:
+                    nc.scalar.activation(y[:, g, :], sums[g][:], identity, bias=biases[h][:, g : g + 1])
+            nc.sync.dma_start(out_rows[h], y[:])

@@ -7,7 +7,7 @@ N = 128
 M = 1024
 CB = C // P
 MB = M // P
-PAIRS = CB // 2
+BANKS = MB // 2
 
 FLOPS = 2 * C * 2 * M * N
 
@@ -31,19 +31,8 @@ def tile_transformerclassifier_kernel(tc, emb, pos, wq, bq, wk, bk, offs, out):
         tc.tile_pool(name="held", bufs=1) as held,
         tc.psum_pool(name="banks", bufs=1) as banks,
     ):
-        def queue_of(i):
-            return nc.sync if i % 2 == 0 else nc.scalar
-
-        def load_weight_pair(h, i):
-            weight = held.tile([P, 2, P, MB], BF16, name=f"weight{h}_{i}")
-            queue_of(i).dma_start(weight[:], weight_rows[h][:, 2 * i : 2 * i + 2])
-            return weight
-
         offsets = held.tile([P, N // 16], U16, name="offsets")
         nc.sync.dma_start(offsets[:], offs)
-
-        pos_sb = held.tile([P, CB, N], F32, name="pos_sb")
-        nc.scalar.dma_start(pos_sb[:], pos_rows)
 
         biases = []
         for h in range(2):
@@ -51,40 +40,50 @@ def tile_transformerclassifier_kernel(tc, emb, pos, wq, bq, wk, bk, offs, out):
             nc.gpsimd.dma_start(bias[:], bias_rows[h])
             biases.append(bias)
 
+        def load_weight_block(h, b):
+            weight = held.tile([P, P, MB], BF16, name=f"weight{h}_{b}")
+            nc.sync.dma_start(weight[:], weight_rows[h][:, b])
+            return weight
+
         tables = []
+        pos_pairs = []
         weights = [[], []]
-        for i in range(PAIRS):
-            for b in (2 * i, 2 * i + 1):
-                table = held.tile([P, S], F32, name=f"table{b}")
-                queue_of(i).dma_start(table[:], emb_blocks[b])
-                tables.append(table)
-            weights[0].append(load_weight_pair(0, i))
-        for i in range(PAIRS):
-            weights[1].append(load_weight_pair(1, i))
+        for b in range(CB):
+            if b % 2 == 0:
+                pos_pair = held.tile([P, 2, N], F32, name=f"pos_pair{b // 2}")
+                nc.sync.dma_start(pos_pair[:], pos_rows[:, b : b + 2])
+                pos_pairs.append(pos_pair)
+            table = held.tile([P, S], F32, name=f"table{b}")
+            nc.sync.dma_start(table[:], emb_blocks[b])
+            tables.append(table)
+            weights[0].append(load_weight_block(0, b))
+        for b in range(CB):
+            weights[1].append(load_weight_block(1, b))
 
         xs = []
         for b in range(CB):
             x_f32 = held.tile([P, N], F32, name=f"x_f32_{b}")
-            nc.vector.tensor_tensor(x_f32[:], tables[b][:].indirect(offsets[:]), pos_sb[:, b, :], add)
+            nc.vector.tensor_tensor(x_f32[:], tables[b][:].indirect(offsets[:]), pos_pairs[b // 2][:, b % 2, :], add)
             x = held.tile([P, N], BF16, name=f"x{b}")
             nc.vector.tensor_copy(x[:], x_f32[:])
             xs.append(x)
 
         for h in range(2):
-            sums = [banks.tile([P, N], F32, name=f"sum{g}") for g in range(MB)]
+            sums = [banks.tile([P, 2, N], F32, name=f"sum{h}_{k}") for k in range(BANKS)]
             for b in range(CB):
                 for g in range(MB):
                     nc.tensor.matmul(
-                        sums[g][:],
-                        weights[h][b // 2][:, b % 2, :, g],
+                        sums[g // 2][:, g % 2, :],
+                        weights[h][b][:, :, g],
                         xs[b][:],
-                        start=(b == 0),
-                        stop=(b == CB - 1),
+                        start=(b == 0 and g % 2 == 0),
+                        stop=(b == CB - 1 and g % 2 == 1),
                     )
-            y = held.tile([P, MB, N], F32, name=f"y{h}")
-            for g in range(MB):
-                if g % 2 == 0:
-                    nc.vector.tensor_scalar(y[:, g, :], sums[g][:], biases[h][:, g : g + 1], None, add)
-                else:
-                    nc.scalar.activation(y[:, g, :], sums[g][:], identity, bias=biases[h][:, g : g + 1])
-            nc.sync.dma_start(out_rows[h], y[:])
+            for k in range(BANKS):
+                y = held.tile([P, 2, N], F32, name=f"y{h}_{k}")
+                for g in (2 * k, 2 * k + 1):
+                    if k % 2 == 0:
+                        nc.vector.tensor_scalar(y[:, g % 2, :], sums[k][:, g % 2, :], biases[h][:, g : g + 1], None, add)
+                    else:
+                        nc.scalar.activation(y[:, g % 2, :], sums[k][:, g % 2, :], identity, bias=biases[h][:, g : g + 1])
+                nc.sync.dma_start(out_rows[h][:, 2 * k : 2 * k + 2], y[:])

@@ -27,6 +27,12 @@ def tile_transformerclassifier_kernel(tc, emb, pos, wq, bq, wk, bk, offs, out):
     bias_rows = [v.rearrange("(p g) o -> p (g o)", g=MB) for v in (bq, bk)]
     out_rows = out.rearrange("(h p g) j -> h p g j", h=2, g=MB)
 
+    pairs = [(b, b + 2) for b in range(0, CB, 2)]
+    pieces_of = [
+        [(0, 1), (1, 2)] + pairs[1:],
+        pairs[:-1] + [(CB - 2, CB - 1), (CB - 1, CB)],
+    ]
+
     with (
         tc.tile_pool(name="held", bufs=1) as held,
         tc.psum_pool(name="banks", bufs=1) as banks,
@@ -34,36 +40,41 @@ def tile_transformerclassifier_kernel(tc, emb, pos, wq, bq, wk, bk, offs, out):
         offsets = held.tile([P, N // 16], U16, name="offsets")
         nc.sync.dma_start(offsets[:], offs)
 
+        weight_of = [{}, {}]
+
+        def load_weight_piece(h, first, end):
+            piece = held.tile([P, end - first, P, MB], BF16, name=f"weight{h}_{first}")
+            nc.sync.dma_start(piece[:], weight_rows[h][:, first:end])
+            for b in range(first, end):
+                weight_of[h][b] = piece[:, b - first]
+
+        pos_head = held.tile([P, 2, N], F32, name="pos_head")
+        pos_rest = held.tile([P, CB - 2, N], F32, name="pos_rest")
+        pos_of = [pos_head[:, b, :] for b in range(2)] + [pos_rest[:, b, :] for b in range(CB - 2)]
+        tables = []
+        nc.sync.dma_start(pos_head[:], pos_rows[:, 0:2])
+        for first, end in pieces_of[0]:
+            if first == 2:
+                nc.sync.dma_start(pos_rest[:], pos_rows[:, 2:CB])
+            for b in range(first, end):
+                table = held.tile([P, S], F32, name=f"table{b}")
+                nc.sync.dma_start(table[:], emb_blocks[b])
+                tables.append(table)
+            load_weight_piece(0, first, end)
+
         biases = []
         for h in range(2):
             bias = held.tile([P, MB], F32, name=f"bias{h}")
             nc.gpsimd.dma_start(bias[:], bias_rows[h])
             biases.append(bias)
 
-        def load_weight_block(h, b):
-            weight = held.tile([P, P, MB], BF16, name=f"weight{h}_{b}")
-            nc.sync.dma_start(weight[:], weight_rows[h][:, b])
-            return weight
-
-        tables = []
-        pos_pairs = []
-        weights = [[], []]
-        for b in range(CB):
-            if b % 2 == 0:
-                pos_pair = held.tile([P, 2, N], F32, name=f"pos_pair{b // 2}")
-                nc.sync.dma_start(pos_pair[:], pos_rows[:, b : b + 2])
-                pos_pairs.append(pos_pair)
-            table = held.tile([P, S], F32, name=f"table{b}")
-            nc.sync.dma_start(table[:], emb_blocks[b])
-            tables.append(table)
-            weights[0].append(load_weight_block(0, b))
-        for b in range(CB):
-            weights[1].append(load_weight_block(1, b))
+        for first, end in pieces_of[1]:
+            load_weight_piece(1, first, end)
 
         xs = []
         for b in range(CB):
             x_f32 = held.tile([P, N], F32, name=f"x_f32_{b}")
-            nc.vector.tensor_tensor(x_f32[:], tables[b][:].indirect(offsets[:]), pos_pairs[b // 2][:, b % 2, :], add)
+            nc.vector.tensor_tensor(x_f32[:], tables[b][:].indirect(offsets[:]), pos_of[b], add)
             x = held.tile([P, N], BF16, name=f"x{b}")
             nc.vector.tensor_copy(x[:], x_f32[:])
             xs.append(x)
@@ -74,16 +85,19 @@ def tile_transformerclassifier_kernel(tc, emb, pos, wq, bq, wk, bk, offs, out):
                 for g in range(MB):
                     nc.tensor.matmul(
                         sums[g // 2][:, g % 2, :],
-                        weights[h][b][:, :, g],
+                        weight_of[h][b][:, :, g],
                         xs[b][:],
                         start=(b == 0 and g % 2 == 0),
                         stop=(b == CB - 1 and g % 2 == 1),
                     )
+            y = held.tile([P, MB, N], F32, name=f"y{h}")
             for k in range(BANKS):
-                y = held.tile([P, 2, N], F32, name=f"y{h}_{k}")
                 for g in (2 * k, 2 * k + 1):
                     if k % 2 == 0:
-                        nc.vector.tensor_scalar(y[:, g % 2, :], sums[k][:, g % 2, :], biases[h][:, g : g + 1], None, add)
+                        nc.vector.tensor_scalar(y[:, g, :], sums[k][:, g % 2, :], biases[h][:, g : g + 1], None, add)
                     else:
-                        nc.scalar.activation(y[:, g % 2, :], sums[k][:, g % 2, :], identity, bias=biases[h][:, g : g + 1])
-                nc.sync.dma_start(out_rows[h][:, 2 * k : 2 * k + 2], y[:])
+                        nc.scalar.activation(y[:, g, :], sums[k][:, g % 2, :], identity, bias=biases[h][:, g : g + 1])
+                if h == 1:
+                    nc.sync.dma_start(out_rows[h][:, 2 * k : 2 * k + 2], y[:, 2 * k : 2 * k + 2, :])
+            if h == 0:
+                nc.sync.dma_start(out_rows[h], y[:])

@@ -27,10 +27,9 @@ def tile_transformerclassifier_kernel(tc, emb, pos, wq, bq, wk, bk, offs, out):
     bias_rows = [v.rearrange("(p g) o -> p (g o)", g=MB) for v in (bq, bk)]
     out_rows = out.rearrange("(h p g) j -> h p g j", h=2, g=MB)
 
-    pairs = [(b, b + 2) for b in range(0, CB, 2)]
     pieces_of = [
-        [(0, 1), (1, 2)] + pairs[1:],
-        pairs[:-1] + [(CB - 2, CB - 1), (CB - 1, CB)],
+        [(0, 4), (4, 6), (6, 8)],
+        [(0, 2), (2, 4), (4, 6), (6, 7), (7, 8)],
     ]
 
     with (
@@ -48,14 +47,10 @@ def tile_transformerclassifier_kernel(tc, emb, pos, wq, bq, wk, bk, offs, out):
             for b in range(first, end):
                 weight_of[h][b] = piece[:, b - first]
 
-        pos_head = held.tile([P, 2, N], F32, name="pos_head")
-        pos_rest = held.tile([P, CB - 2, N], F32, name="pos_rest")
-        pos_of = [pos_head[:, b, :] for b in range(2)] + [pos_rest[:, b, :] for b in range(CB - 2)]
+        pos_sb = held.tile([P, CB, N], F32, name="pos_sb")
+        nc.sync.dma_start(pos_sb[:], pos_rows)
         tables = []
-        nc.sync.dma_start(pos_head[:], pos_rows[:, 0:2])
         for first, end in pieces_of[0]:
-            if first == 2:
-                nc.sync.dma_start(pos_rest[:], pos_rows[:, 2:CB])
             for b in range(first, end):
                 table = held.tile([P, S], F32, name=f"table{b}")
                 nc.sync.dma_start(table[:], emb_blocks[b])
@@ -74,7 +69,7 @@ def tile_transformerclassifier_kernel(tc, emb, pos, wq, bq, wk, bk, offs, out):
         xs = []
         for b in range(CB):
             x_f32 = held.tile([P, N], F32, name=f"x_f32_{b}")
-            nc.vector.tensor_tensor(x_f32[:], tables[b][:].indirect(offsets[:]), pos_of[b], add)
+            nc.vector.tensor_tensor(x_f32[:], tables[b][:].indirect(offsets[:]), pos_sb[:, b, :], add)
             x = held.tile([P, N], BF16, name=f"x{b}")
             nc.vector.tensor_copy(x[:], x_f32[:])
             xs.append(x)

@@ -21,14 +21,14 @@ def tile_transformerclassifier_kernel(tc, emb, pos, wq, bq, wk, bk, offs, out):
     add = mybir.AluOpType.add
     identity = mybir.ActivationFunctionType.Identity
 
-    emb_blocks = emb.rearrange("(p b) s -> b p s", b=CB)
+    emb_rows = emb.rearrange("(p b) s -> p b s", b=CB)
     pos_rows = pos.rearrange("(p b) j -> p b j", b=CB)
     weight_rows = [w.rearrange("(p b) (m g) -> p b m g", b=CB, g=MB) for w in (wq, wk)]
     bias_rows = [v.rearrange("(p g) o -> p (g o)", g=MB) for v in (bq, bk)]
     out_rows = out.rearrange("(h p g) j -> h p g j", h=2, g=MB)
 
     pieces_of = [
-        [(0, 4), (4, 6), (6, 8)],
+        [(0, 2), (2, 4), (4, 6), (6, 8)],
         [(0, 2), (2, 4), (4, 6), (6, 7), (7, 8)],
     ]
 
@@ -49,12 +49,12 @@ def tile_transformerclassifier_kernel(tc, emb, pos, wq, bq, wk, bk, offs, out):
 
         pos_sb = held.tile([P, CB, N], F32, name="pos_sb")
         nc.sync.dma_start(pos_sb[:], pos_rows)
-        tables = []
+        emb_halves = []
         for first, end in pieces_of[0]:
-            for b in range(first, end):
-                table = held.tile([P, S], F32, name=f"table{b}")
-                nc.sync.dma_start(table[:], emb_blocks[b])
-                tables.append(table)
+            if first % 4 == 0:
+                emb_half = held.tile([P, 4, S], F32, name=f"emb{first}")
+                nc.sync.dma_start(emb_half[:], emb_rows[:, first : first + 4])
+                emb_halves.append(emb_half)
             load_weight_piece(0, first, end)
 
         biases = []
@@ -68,8 +68,10 @@ def tile_transformerclassifier_kernel(tc, emb, pos, wq, bq, wk, bk, offs, out):
 
         xs = []
         for b in range(CB):
+            table = held.tile([P, S], F32, name=f"table{b}")
+            nc.vector.tensor_copy(table[:], emb_halves[b // 4][:, b % 4, :])
             x_f32 = held.tile([P, N], F32, name=f"x_f32_{b}")
-            nc.vector.tensor_tensor(x_f32[:], tables[b][:].indirect(offsets[:]), pos_sb[:, b, :], add)
+            nc.vector.tensor_tensor(x_f32[:], table[:].indirect(offsets[:]), pos_sb[:, b, :], add)
             x = held.tile([P, N], BF16, name=f"x{b}")
             nc.vector.tensor_copy(x[:], x_f32[:])
             xs.append(x)

@@ -27,9 +27,9 @@ def tile_transformerclassifier_kernel(tc, emb, pos, wq, bq, wk, bk, offs, out):
     bias_rows = [v.rearrange("(p g) o -> p (g o)", g=MB) for v in (bq, bk)]
     out_rows = out.rearrange("(h p g) j -> h p g j", h=2, g=MB)
 
-    pieces_of = [
-        [(0, 2), (2, 4), (4, 6), (6, 8)],
-        [(0, 2), (2, 4), (4, 6), (6, 7), (7, 8)],
+    pieces = [
+        (0, 0, 2), (0, 2, 4), (1, 0, 2), (0, 4, 6), (0, 6, 8),
+        (1, 2, 4), (1, 4, 6), (1, 6, 7), (1, 7, 8),
     ]
 
     with (
@@ -47,15 +47,21 @@ def tile_transformerclassifier_kernel(tc, emb, pos, wq, bq, wk, bk, offs, out):
             for b in range(first, end):
                 weight_of[h][b] = piece[:, b - first]
 
+        emb_of = []
+
+        def load_emb_piece(first, end):
+            piece = held.tile([P, end - first, S], F32, name=f"emb{first}")
+            nc.sync.dma_start(piece[:], emb_rows[:, first:end])
+            for b in range(first, end):
+                emb_of.append(piece[:, b - first, :])
+
         pos_sb = held.tile([P, CB, N], F32, name="pos_sb")
         nc.sync.dma_start(pos_sb[:], pos_rows)
-        emb_halves = []
-        for first, end in pieces_of[0]:
-            if first % 4 == 0:
-                emb_half = held.tile([P, 4, S], F32, name=f"emb{first}")
-                nc.sync.dma_start(emb_half[:], emb_rows[:, first : first + 4])
-                emb_halves.append(emb_half)
-            load_weight_piece(0, first, end)
+        load_emb_piece(0, 2)
+        load_weight_piece(*pieces[0])
+        load_emb_piece(2, CB)
+        for piece in pieces[1:]:
+            load_weight_piece(*piece)
 
         biases = []
         for h in range(2):
@@ -63,37 +69,38 @@ def tile_transformerclassifier_kernel(tc, emb, pos, wq, bq, wk, bk, offs, out):
             nc.gpsimd.dma_start(bias[:], bias_rows[h])
             biases.append(bias)
 
-        for first, end in pieces_of[1]:
-            load_weight_piece(1, first, end)
-
         xs = []
         for b in range(CB):
             table = held.tile([P, S], F32, name=f"table{b}")
-            nc.vector.tensor_copy(table[:], emb_halves[b // 4][:, b % 4, :])
+            nc.vector.tensor_copy(table[:], emb_of[b])
             x_f32 = held.tile([P, N], F32, name=f"x_f32_{b}")
             nc.vector.tensor_tensor(x_f32[:], table[:].indirect(offsets[:]), pos_sb[:, b, :], add)
             x = held.tile([P, N], BF16, name=f"x{b}")
             nc.vector.tensor_copy(x[:], x_f32[:])
             xs.append(x)
 
-        for h in range(2):
-            sums = [banks.tile([P, 2, N], F32, name=f"sum{h}_{k}") for k in range(BANKS)]
-            for b in range(CB):
+        sums = [[banks.tile([P, 2, N], F32, name=f"sum{h}_{k}") for k in range(BANKS)] for h in range(2)]
+        for h, first, end in pieces:
+            for b in range(first, end):
                 for g in range(MB):
                     nc.tensor.matmul(
-                        sums[g // 2][:, g % 2, :],
+                        sums[h][g // 2][:, g % 2, :],
                         weight_of[h][b][:, :, g],
                         xs[b][:],
                         start=(b == 0 and g % 2 == 0),
                         stop=(b == CB - 1 and g % 2 == 1),
                     )
+            if end < CB:
+                continue
             y = held.tile([P, MB, N], F32, name=f"y{h}")
             for k in range(BANKS):
                 for g in (2 * k, 2 * k + 1):
+                    total = sums[h][k][:, g % 2, :]
+                    bias = biases[h][:, g : g + 1]
                     if k % 2 == 0:
-                        nc.vector.tensor_scalar(y[:, g, :], sums[k][:, g % 2, :], biases[h][:, g : g + 1], None, add)
+                        nc.vector.tensor_scalar(y[:, g, :], total, bias, None, add)
                     else:
-                        nc.scalar.activation(y[:, g, :], sums[k][:, g % 2, :], identity, bias=biases[h][:, g : g + 1])
+                        nc.scalar.activation(y[:, g, :], total, identity, bias=bias)
                 if h == 1:
                     nc.sync.dma_start(out_rows[h][:, 2 * k : 2 * k + 2], y[:, 2 * k : 2 * k + 2, :])
             if h == 0:

@@ -7,7 +7,6 @@ N = 128
 M = 1024
 CB = C // P
 MB = M // P
-BANKS = MB // 2
 
 FLOPS = 2 * C * 2 * M * N
 
@@ -28,8 +27,12 @@ def tile_transformerclassifier_kernel(tc, emb, pos, wq, bq, wk, bk, offs, out):
     out_rows = out.rearrange("(h p g) j -> h p g j", h=2, g=MB)
 
     pieces = [
-        (0, 0, 2), (0, 2, 4), (1, 0, 2), (0, 4, 6), (0, 6, 8),
-        (1, 2, 4), (1, 4, 6), (1, 6, 7), (1, 7, 8),
+        (0, 0, 2), (0, 2, 4), (0, 4, 6), (0, 6, 8),
+        (1, 0, 2), (1, 2, 4), (1, 4, 6), (1, 6, 8),
+    ]
+    banks_of = [
+        [(0, 4), (4, 8)],
+        [(0, 2), (2, 4), (4, 5), (5, 6), (6, 7), (7, 8)],
     ]
 
     with (
@@ -57,11 +60,10 @@ def tile_transformerclassifier_kernel(tc, emb, pos, wq, bq, wk, bk, offs, out):
 
         pos_sb = held.tile([P, CB, N], F32, name="pos_sb")
         nc.sync.dma_start(pos_sb[:], pos_rows)
-        load_emb_piece(0, 2)
-        load_weight_piece(*pieces[0])
-        load_emb_piece(2, CB)
-        for piece in pieces[1:]:
-            load_weight_piece(*piece)
+        for h, first, end in pieces:
+            if h == 0:
+                load_emb_piece(first, end)
+            load_weight_piece(h, first, end)
 
         biases = []
         for h in range(2):
@@ -79,29 +81,35 @@ def tile_transformerclassifier_kernel(tc, emb, pos, wq, bq, wk, bk, offs, out):
             nc.vector.tensor_copy(x[:], x_f32[:])
             xs.append(x)
 
-        sums = [[banks.tile([P, 2, N], F32, name=f"sum{h}_{k}") for k in range(BANKS)] for h in range(2)]
-        for h, first, end in pieces:
-            for b in range(first, end):
-                for g in range(MB):
-                    nc.tensor.matmul(
-                        sums[h][g // 2][:, g % 2, :],
-                        weight_of[h][b][:, :, g],
-                        xs[b][:],
-                        start=(b == 0 and g % 2 == 0),
-                        stop=(b == CB - 1 and g % 2 == 1),
-                    )
-            if end < CB:
-                continue
+        for h in range(2):
+            sum_of = []
+            opens = [g for g, end in banks_of[h]]
+            closes = [end - 1 for g, end in banks_of[h]]
+            for first, end in banks_of[h]:
+                bank = banks.tile([P, end - first, N], F32, name=f"sum{h}_{first}")
+                for g in range(first, end):
+                    sum_of.append(bank[:, g - first, :])
+
+            late_blocks = range(CB if h == 0 else CB - 2, CB)
+            products = [(b, g) for b in range(late_blocks.start) for g in range(MB)]
+            products += [(b, g) for g in range(MB) for b in late_blocks]
+            for b, g in products:
+                nc.tensor.matmul(
+                    sum_of[g],
+                    weight_of[h][b][:, :, g],
+                    xs[b][:],
+                    start=(b == 0 and g in opens),
+                    stop=(b == CB - 1 and g in closes),
+                )
+
             y = held.tile([P, MB, N], F32, name=f"y{h}")
-            for k in range(BANKS):
-                for g in (2 * k, 2 * k + 1):
-                    total = sums[h][k][:, g % 2, :]
+            for k, (first, end) in enumerate(banks_of[h]):
+                for g in range(first, end):
                     bias = biases[h][:, g : g + 1]
                     if k % 2 == 0:
-                        nc.vector.tensor_scalar(y[:, g, :], total, bias, None, add)
+                        nc.vector.tensor_scalar(y[:, g, :], sum_of[g], bias, None, add)
                     else:
-                        nc.scalar.activation(y[:, g, :], total, identity, bias=bias)
-                if h == 1:
-                    nc.sync.dma_start(out_rows[h][:, 2 * k : 2 * k + 2], y[:, 2 * k : 2 * k + 2, :])
-            if h == 0:
-                nc.sync.dma_start(out_rows[h], y[:])
+                        nc.scalar.activation(y[:, g, :], sum_of[g], identity, bias=bias)
+            store_width = MB if h == 0 else 2
+            for g in range(0, MB, store_width):
+                nc.sync.dma_start(out_rows[h][:, g : g + store_width], y[:, g : g + store_width, :])

import concourse.mybir as mybir

P = 128
C = 1024
S = 256
N = 128
M = 1024
CB = C // P
MB = M // P

FLOPS = 2 * C * 2 * M * N

F32 = mybir.dt.float32
BF16 = mybir.dt.bfloat16
U16 = mybir.dt.uint16


def tile_transformerclassifier_kernel(tc, emb, pos, wq, bq, wk, bk, offs, out):
    nc = tc.nc
    add = mybir.AluOpType.add
    identity = mybir.ActivationFunctionType.Identity

    emb_rows = emb.rearrange("(p b) s -> p b s", b=CB)
    pos_rows = pos.rearrange("(p b) j -> p b j", b=CB)
    weight_rows = [w.rearrange("(p b) (m g) -> p b m g", b=CB, g=MB) for w in (wq, wk)]
    bias_rows = [v.rearrange("(p g) o -> p (g o)", g=MB) for v in (bq, bk)]
    out_rows = out.rearrange("(h p g) j -> h p g j", h=2, g=MB)

    pieces = [
        (0, 0, 2), (0, 2, 4), (0, 4, 6), (0, 6, 8),
        (1, 0, 2), (1, 2, 4), (1, 4, 6), (1, 6, 8),
    ]
    banks_of = [
        [(0, 4), (4, 8)],
        [(0, 2), (2, 4), (4, 5), (5, 6), (6, 7), (7, 8)],
    ]

    with (
        tc.tile_pool(name="held", bufs=1) as held,
        tc.psum_pool(name="banks", bufs=1) as banks,
    ):
        offsets = held.tile([P, N // 16], U16, name="offsets")
        nc.sync.dma_start(offsets[:], offs)

        weight_of = [{}, {}]

        def load_weight_piece(h, first, end):
            piece = held.tile([P, end - first, P, MB], BF16, name=f"weight{h}_{first}")
            nc.sync.dma_start(piece[:], weight_rows[h][:, first:end])
            for b in range(first, end):
                weight_of[h][b] = piece[:, b - first]

        emb_of = []

        def load_emb_piece(first, end):
            piece = held.tile([P, end - first, S], F32, name=f"emb{first}")
            nc.sync.dma_start(piece[:], emb_rows[:, first:end])
            for b in range(first, end):
                emb_of.append(piece[:, b - first, :])

        pos_sb = held.tile([P, CB, N], F32, name="pos_sb")
        nc.sync.dma_start(pos_sb[:], pos_rows)
        for h, first, end in pieces:
            if h == 0:
                load_emb_piece(first, end)
            load_weight_piece(h, first, end)

        biases = []
        for h in range(2):
            bias = held.tile([P, MB], F32, name=f"bias{h}")
            nc.gpsimd.dma_start(bias[:], bias_rows[h])
            biases.append(bias)

        xs = []
        for b in range(CB):
            table = held.tile([P, S], F32, name=f"table{b}")
            nc.vector.tensor_copy(table[:], emb_of[b])
            x_f32 = held.tile([P, N], F32, name=f"x_f32_{b}")
            nc.vector.tensor_tensor(x_f32[:], table[:].indirect(offsets[:]), pos_sb[:, b, :], add)
            x = held.tile([P, N], BF16, name=f"x{b}")
            nc.vector.tensor_copy(x[:], x_f32[:])
            xs.append(x)

        for h in range(2):
            sum_of = []
            opens = [g for g, end in banks_of[h]]
            closes = [end - 1 for g, end in banks_of[h]]
            for first, end in banks_of[h]:
                bank = banks.tile([P, end - first, N], F32, name=f"sum{h}_{first}")
                for g in range(first, end):
                    sum_of.append(bank[:, g - first, :])

            late_blocks = range(CB if h == 0 else CB - 2, CB)
            products = [(b, g) for b in range(late_blocks.start) for g in range(MB)]
            products += [(b, g) for g in range(MB) for b in late_blocks]
            for b, g in products:
                nc.tensor.matmul(
                    sum_of[g],
                    weight_of[h][b][:, :, g],
                    xs[b][:],
                    start=(b == 0 and g in opens),
                    stop=(b == CB - 1 and g in closes),
                )

            y = held.tile([P, MB, N], F32, name=f"y{h}")
            for k, (first, end) in enumerate(banks_of[h]):
                for g in range(first, end):
                    bias = biases[h][:, g : g + 1]
                    if k % 2 == 0:
                        nc.vector.tensor_scalar(y[:, g, :], sum_of[g], bias, None, add)
                    else:
                        nc.scalar.activation(y[:, g, :], sum_of[g], identity, bias=bias)
            store_width = MB if h == 0 else 2
            for g in range(0, MB, store_width):
                nc.sync.dma_start(out_rows[h][:, g : g + store_width], y[:, g : g + store_width, :])
